import numpy as np
import ml_dtypes

BF16 = ml_dtypes.bfloat16


def bf(x):
    return np.asarray(x, np.float32).astype(BF16)


def f32(x):
    return np.asarray(x, np.float32)


def f64(x):
    return np.asarray(x).astype(np.float64)


def striped(idx):
    return np.tile(idx.reshape(-1, 16).T, (8, 1))


D, S, Q, N = 128, 2048, 256, 256


def position_encoding():
    i = np.arange(1, D + 1, dtype=np.float64)[:, None]
    return 1.0 + 4.0 * (i - D / 2.0) * 0.5 / D


def setup_inputs():
    return {"table": bf(0.5 * np.random.standard_normal((D, S))), "q": bf(0.15 * np.random.standard_normal((D, Q))), "enc": f32(position_encoding()), "offs": striped(np.random.permutation(np.tile(np.arange(S), 2))[:N])}


def reference(table, q, enc, offs):
    idx = offs[:16].T.reshape(-1)
    w = f64(enc) ** 2 * f64(q)
    score = w.T @ f64(table)[:, idx]
    e = np.exp(score - score.max(axis=1, keepdims=True))
    return e / e.sum(axis=1, keepdims=True)

@@ -1,0 +1,51 @@
+import concourse.mybir as mybir
+
+BF16, F32, U16 = mybir.dt.bfloat16, mybir.dt.float32, mybir.dt.uint16
+MULT, MAX = mybir.AluOpType.mult, mybir.AluOpType.max
+EXP = mybir.ActivationFunctionType.Exp
+ALONG_ROW = mybir.AxisListType.X
+
+D = 128
+S = 2048
+Q = 256
+N = 256
+BLOCK = 128
+
+FLOPS = 2 * D * Q * N
+
+
+def tile_memn2n_kernel(tc, table, q, enc, offs, out):
+    nc = tc.nc
+    with (
+        tc.tile_pool(name="held", bufs=1) as held,
+        tc.tile_pool(name="work", bufs=2) as work,
+        tc.psum_pool(name="psum", bufs=2) as psum,
+    ):
+        offsets = held.tile([D, N // 16], U16, name="offsets")
+        nc.sync.dma_start(offsets[:], offs)
+        words = held.tile([D, S], BF16, name="words")
+        nc.sync.dma_start(words[:], table)
+        queries = held.tile([D, Q], BF16, name="queries")
+        nc.sync.dma_start(queries[:], q)
+        encoding = held.tile([D, 1], F32, name="encoding")
+        nc.sync.dma_start(encoding[:], enc)
+
+        weights = held.tile([D, Q], BF16, name="weights")
+        nc.vector.tensor_scalar(weights[:], queries[:], encoding[:], encoding[:], MULT, MULT)
+
+        for b in range(Q // BLOCK):
+            rows = slice(b * BLOCK, (b + 1) * BLOCK)
+
+            score = psum.tile([BLOCK, N], F32, name="score")
+            nc.tensor.matmul(score[:], weights[:, rows], words[:].indirect(offsets[:]), start=True, stop=True)
+
+            minus_max = work.tile([BLOCK, 1], F32, name="minus_max")
+            nc.vector.tensor_reduce(minus_max[:], score[:], ALONG_ROW, MAX, negate=True)
+            expd = work.tile([BLOCK, N], F32, name="expd")
+            total = work.tile([BLOCK, 1], F32, name="total")
+            nc.scalar.activation(expd[:], score[:], EXP, bias=minus_max[:], scale=1.0, accum_out=total[:])
+            inverse = work.tile([BLOCK, 1], F32, name="inverse")
+            nc.vector.reciprocal(inverse[:], total[:])
+            probs = work.tile([BLOCK, N], F32, name="probs")
+            nc.vector.tensor_scalar_mul(probs[:], expd[:], inverse[:])
+            nc.sync.dma_start(out[rows, :], probs[:])

@@ -21,14 +21,14 @@ def tile_memn2n_kernel(tc, table, q, enc, offs, out):
         tc.tile_pool(name="work", bufs=2) as work,
         tc.psum_pool(name="psum", bufs=2) as psum,
     ):
-        offsets = held.tile([D, N // 16], U16, name="offsets")
-        nc.sync.dma_start(offsets[:], offs)
         words = held.tile([D, S], BF16, name="words")
         nc.sync.dma_start(words[:], table)
-        queries = held.tile([D, Q], BF16, name="queries")
-        nc.sync.dma_start(queries[:], q)
+        offsets = held.tile([D, N // 16], U16, name="offsets")
+        nc.sync.dma_start(offsets[:], offs)
         encoding = held.tile([D, 1], F32, name="encoding")
-        nc.sync.dma_start(encoding[:], enc)
+        nc.scalar.dma_start(encoding[:], enc)
+        queries = held.tile([D, Q], BF16, name="queries")
+        nc.scalar.dma_start(queries[:], q)
 
         weights = held.tile([D, Q], BF16, name="weights")
         nc.vector.tensor_scalar(weights[:], queries[:], encoding[:], encoding[:], MULT, MULT)
@@ -48,4 +48,5 @@ def tile_memn2n_kernel(tc, table, q, enc, offs, out):
             nc.vector.reciprocal(inverse[:], total[:])
             probs = work.tile([BLOCK, N], F32, name="probs")
             nc.vector.tensor_scalar_mul(probs[:], expd[:], inverse[:])
-            nc.sync.dma_start(out[rows, :], probs[:])
+            store_queue = (nc.sync, nc.scalar)[b]
+            store_queue.dma_start(out[rows, :], probs[:])

@@ -21,14 +21,14 @@ def tile_memn2n_kernel(tc, table, q, enc, offs, out):
         tc.tile_pool(name="work", bufs=2) as work,
         tc.psum_pool(name="psum", bufs=2) as psum,
     ):
-        words = held.tile([D, S], BF16, name="words")
-        nc.sync.dma_start(words[:], table)
+        encoding = held.tile([D, 1], F32, name="encoding")
+        nc.sync.dma_start(encoding[:], enc)
+        queries = held.tile([D, Q], BF16, name="queries")
+        nc.sync.dma_start(queries[:], q)
         offsets = held.tile([D, N // 16], U16, name="offsets")
         nc.sync.dma_start(offsets[:], offs)
-        encoding = held.tile([D, 1], F32, name="encoding")
-        nc.scalar.dma_start(encoding[:], enc)
-        queries = held.tile([D, Q], BF16, name="queries")
-        nc.scalar.dma_start(queries[:], q)
+        words = held.tile([D, S], BF16, name="words")
+        nc.sync.dma_start(words[:], table)
 
         weights = held.tile([D, Q], BF16, name="weights")
         nc.vector.tensor_scalar(weights[:], queries[:], encoding[:], encoding[:], MULT, MULT)
@@ -48,5 +48,4 @@ def tile_memn2n_kernel(tc, table, q, enc, offs, out):
             nc.vector.reciprocal(inverse[:], total[:])
             probs = work.tile([BLOCK, N], F32, name="probs")
             nc.vector.tensor_scalar_mul(probs[:], expd[:], inverse[:])
-            store_queue = (nc.sync, nc.scalar)[b]
-            store_queue.dma_start(out[rows, :], probs[:])
+            nc.sync.dma_start(out[rows, :], probs[:])

@@ -25,10 +25,10 @@ def tile_memn2n_kernel(tc, table, q, enc, offs, out):
         nc.sync.dma_start(encoding[:], enc)
         queries = held.tile([D, Q], BF16, name="queries")
         nc.sync.dma_start(queries[:], q)
-        offsets = held.tile([D, N // 16], U16, name="offsets")
-        nc.sync.dma_start(offsets[:], offs)
         words = held.tile([D, S], BF16, name="words")
         nc.sync.dma_start(words[:], table)
+        offsets = held.tile([D, N // 16], U16, name="offsets")
+        nc.sync.dma_start(offsets[:], offs)
 
         weights = held.tile([D, Q], BF16, name="weights")
         nc.vector.tensor_scalar(weights[:], queries[:], encoding[:], encoding[:], MULT, MULT)

@@ -30,6 +30,11 @@ def tile_memn2n_kernel(tc, table, q, enc, offs, out):
         offsets = held.tile([D, N // 16], U16, name="offsets")
         nc.sync.dma_start(offsets[:], offs)
 
+        zero = held.tile([D, 1], F32, name="zero")
+        nc.vector.memset(zero[:], 0.0)
+        warm = held.tile([D, 1], F32, name="warm")
+        nc.scalar.activation(warm[:], zero[:], EXP)
+
         weights = held.tile([D, Q], BF16, name="weights")
         nc.vector.tensor_scalar(weights[:], queries[:], encoding[:], encoding[:], MULT, MULT)
 

import concourse.mybir as mybir

BF16, F32, U16 = mybir.dt.bfloat16, mybir.dt.float32, mybir.dt.uint16
MULT, MAX = mybir.AluOpType.mult, mybir.AluOpType.max
EXP = mybir.ActivationFunctionType.Exp
ALONG_ROW = mybir.AxisListType.X

D = 128
S = 2048
Q = 256
N = 256
BLOCK = 128

FLOPS = 2 * D * Q * N


def tile_memn2n_kernel(tc, table, q, enc, offs, out):
    nc = tc.nc
    with (
        tc.tile_pool(name="held", bufs=1) as held,
        tc.tile_pool(name="work", bufs=2) as work,
        tc.psum_pool(name="psum", bufs=2) as psum,
    ):
        encoding = held.tile([D, 1], F32, name="encoding")
        nc.sync.dma_start(encoding[:], enc)
        queries = held.tile([D, Q], BF16, name="queries")
        nc.sync.dma_start(queries[:], q)
        words = held.tile([D, S], BF16, name="words")
        nc.sync.dma_start(words[:], table)
        offsets = held.tile([D, N // 16], U16, name="offsets")
        nc.sync.dma_start(offsets[:], offs)

        zero = held.tile([D, 1], F32, name="zero")
        nc.vector.memset(zero[:], 0.0)
        warm = held.tile([D, 1], F32, name="warm")
        nc.scalar.activation(warm[:], zero[:], EXP)

        weights = held.tile([D, Q], BF16, name="weights")
        nc.vector.tensor_scalar(weights[:], queries[:], encoding[:], encoding[:], MULT, MULT)

        for b in range(Q // BLOCK):
            rows = slice(b * BLOCK, (b + 1) * BLOCK)

            score = psum.tile([BLOCK, N], F32, name="score")
            nc.tensor.matmul(score[:], weights[:, rows], words[:].indirect(offsets[:]), start=True, stop=True)

            minus_max = work.tile([BLOCK, 1], F32, name="minus_max")
            nc.vector.tensor_reduce(minus_max[:], score[:], ALONG_ROW, MAX, negate=True)
            expd = work.tile([BLOCK, N], F32, name="expd")
            total = work.tile([BLOCK, 1], F32, name="total")
            nc.scalar.activation(expd[:], score[:], EXP, bias=minus_max[:], scale=1.0, accum_out=total[:])
            inverse = work.tile([BLOCK, 1], F32, name="inverse")
            nc.vector.reciprocal(inverse[:], total[:])
            probs = work.tile([BLOCK, N], F32, name="probs")
            nc.vector.tensor_scalar_mul(probs[:], expd[:], inverse[:])
            nc.sync.dma_start(out[rows, :], probs[:])
